import numpy as np
import ml_dtypes

BF16 = ml_dtypes.bfloat16


def bf(x):
    return np.asarray(x, np.float32).astype(BF16)


def f32(x):
    return np.asarray(x, np.float32)


def f64(x):
    return np.asarray(x).astype(np.float64)


def striped(idx):
    return np.tile(idx.reshape(-1, 16).T, (8, 1))


C, S, N, E = 256, 4096, 1024, 128
GATE = 1.0
EPS = 1e-08


def softmax_rows(v):
    ex = np.exp(v - v.max(axis=1, keepdims=True))
    return ex / ex.sum(axis=1, keepdims=True)


def setup_inputs():
    return {"base": f32(np.random.standard_normal((C, S))), "q": bf(np.random.standard_normal((E, C))), "k": bf(np.random.standard_normal((E, N))), "offs": striped(np.random.permutation(S)[:N])}


def reference(base, q, k, offs):
    idx = offs[:16].T.reshape(-1)
    q, k = f64(q), f64(k)
    sc = 1.0 / np.sqrt(E)
    dot = q.T @ k
    qn = np.sum(q**2, axis=0)[:, None]
    kn = np.sum(k**2, axis=0)[None, :]
    wed = np.sqrt(np.maximum(qn * kn - dot**2, 0.0) + EPS)
    mix = 1.0 / (1.0 + np.exp(-GATE))
    out = f64(base).copy()
    out[:, idx] = (1.0 - mix) * (N * softmax_rows(sc * dot)) + mix * (N * softmax_rows(sc * wed))
    return out

@@ -1,0 +1,152 @@
+import math
+
+import concourse.mybir as mybir
+
+F32 = mybir.dt.float32
+BF16 = mybir.dt.bfloat16
+U16 = mybir.dt.uint16
+ALU = mybir.AluOpType
+FUNC = mybir.ActivationFunctionType
+AXIS = mybir.AxisListType
+
+P = 128
+C, S, N, E = 256, 4096, 1024, 128
+BLOCKS = C // P
+BANK = 512
+HALVES = N // BANK
+SC = 1.0 / math.sqrt(E)
+MIX = 1.0 / (1.0 + math.exp(-1.0))
+EPS = 1e-8
+
+FLOPS = 2 * C * N * E
+
+
+def tile_dualpathgeomattention_kernel(tc, base, q, k, offs, out):
+    nc = tc.nc
+    with (
+        tc.tile_pool(name="held", bufs=1) as held,
+        tc.psum_pool(name="psum", bufs=1) as psum,
+    ):
+        q_sb = held.tile([E, C], BF16, name="q_sb")
+        k_sb = held.tile([E, N], BF16, name="k_sb")
+        offsets = held.tile([P, N // 16], U16, name="offsets")
+        nc.sync.dma_start(q_sb[:], q)
+        nc.sync.dma_start(k_sb[:], k)
+        nc.sync.dma_start(offsets[:], offs)
+        windows = []
+        for b in range(BLOCKS):
+            window = held.tile([P, S], F32, name=f"window{b}")
+            nc.sync.dma_start(window[:], base[b * P : (b + 1) * P, :])
+            windows.append(window)
+
+        ones = held.tile([E, P], BF16, name="ones")
+        nc.gpsimd.memset(ones[:], 1.0)
+        eps_col = held.tile([P, 1], F32, name="eps_col")
+        nc.gpsimd.memset(eps_col[:], EPS)
+
+        q_sq = held.tile([E, C], BF16, name="q_sq")
+        k_sq = held.tile([E, N], BF16, name="k_sq")
+        nc.vector.tensor_tensor(q_sq[:], q_sb[:], q_sb[:], ALU.mult)
+        nc.vector.tensor_tensor(k_sq[:], k_sb[:], k_sb[:], ALU.mult)
+
+        dot_ps = [
+            [psum.tile([P, BANK], F32, name=f"dot_ps{b}{h}") for h in range(HALVES)]
+            for b in range(BLOCKS)
+        ]
+        for b in range(BLOCKS):
+            for h in range(HALVES):
+                nc.tensor.matmul(
+                    dot_ps[b][h][:],
+                    q_sb[:, b * P : (b + 1) * P],
+                    k_sb[:, h * BANK : (h + 1) * BANK],
+                    start=True,
+                    stop=True,
+                )
+        qn_ps = psum.tile([P, BLOCKS], F32, name="qn_ps")
+        for b in range(BLOCKS):
+            nc.tensor.matmul(
+                qn_ps[:, b : b + 1], q_sq[:, b * P : (b + 1) * P], ones[:, 0:1], start=True, stop=True
+            )
+        qn = held.tile([P, BLOCKS], F32, name="qn")
+        nc.vector.tensor_copy(qn[:], qn_ps[:])
+        kn_ps = [psum.tile([P, BANK], F32, name=f"kn_ps{h}") for h in range(HALVES)]
+        for h in range(HALVES):
+            nc.tensor.matmul(
+                kn_ps[h][:], ones[:], k_sq[:, h * BANK : (h + 1) * BANK], start=True, stop=True
+            )
+
+        dot_sq = [held.tile([P, N], F32, name=f"dot_sq{b}") for b in range(BLOCKS)]
+        for b in range(BLOCKS):
+            for h in range(HALVES):
+                cols = slice(h * BANK, (h + 1) * BANK)
+                nc.scalar.activation(dot_sq[b][:, cols], dot_ps[b][h][:], FUNC.Square)
+
+        wed = []
+        wed_shift = []
+        for b in range(BLOCKS):
+            gram = held.tile([P, N], F32, name=f"gram{b}")
+            clamped = held.tile([P, N], F32, name=f"clamped{b}")
+            clamped_top = held.tile([P, HALVES], F32, name=f"clamped_top{b}")
+            wed_b = held.tile([P, N], F32, name=f"wed{b}")
+            for h in range(HALVES):
+                cols = slice(h * BANK, (h + 1) * BANK)
+                nc.vector.scalar_tensor_tensor(
+                    gram[:, cols], kn_ps[h][:], qn[:, b : b + 1], dot_sq[b][:, cols], ALU.mult, ALU.subtract
+                )
+            for h in range(HALVES):
+                cols = slice(h * BANK, (h + 1) * BANK)
+                nc.vector.tensor_scalar(
+                    clamped[:, cols], gram[:, cols], 0.0, None, ALU.max, ALU.max,
+                    accum_out=clamped_top[:, h : h + 1],
+                )
+                nc.scalar.activation(wed_b[:, cols], clamped[:, cols], FUNC.Sqrt, bias=eps_col[:])
+            row_top = held.tile([P, 1], F32, name=f"row_top{b}")
+            wed_top = held.tile([P, 1], F32, name=f"wed_top{b}")
+            shift = held.tile([P, 1], F32, name=f"wed_shift{b}")
+            nc.vector.tensor_tensor(row_top[:], clamped_top[:, 0:1], clamped_top[:, 1:2], ALU.max)
+            nc.scalar.activation(wed_top[:], row_top[:], FUNC.Sqrt, bias=eps_col[:])
+            nc.vector.tensor_scalar_mul(shift[:], wed_top[:], -SC)
+            wed.append(wed_b)
+            wed_shift.append(shift)
+
+        dot_shift = []
+        for b in range(BLOCKS):
+            dot_top = held.tile([P, HALVES], F32, name=f"dot_top{b}")
+            shift = held.tile([P, 1], F32, name=f"dot_shift{b}")
+            for h in range(HALVES):
+                nc.vector.reduce_max(dot_top[:, h : h + 1], dot_ps[b][h][:], axis=AXIS.X)
+            nc.vector.tensor_scalar(
+                shift[:], dot_top[:, 0:1], dot_top[:, 1:2], -SC, ALU.max, ALU.mult
+            )
+            dot_shift.append(shift)
+
+        for b in range(BLOCKS):
+            dot_exp = held.tile([P, N], F32, name=f"dot_exp{b}")
+            wed_exp = held.tile([P, N], F32, name=f"wed_exp{b}")
+            dot_sum2 = held.tile([P, HALVES], F32, name=f"dot_sum2{b}")
+            dot_sum = held.tile([P, 1], F32, name=f"dot_sum{b}")
+            wed_sum = held.tile([P, 1], F32, name=f"wed_sum{b}")
+            for h in range(HALVES):
+                cols = slice(h * BANK, (h + 1) * BANK)
+                nc.scalar.activation(
+                    dot_exp[:, cols], dot_ps[b][h][:], FUNC.Exp, bias=dot_shift[b][:], scale=SC,
+                    accum_out=dot_sum2[:, h : h + 1],
+                )
+            nc.scalar.activation(
+                wed_exp[:], wed[b][:], FUNC.Exp, bias=wed_shift[b][:], scale=SC, accum_out=wed_sum[:]
+            )
+            dot_inv = held.tile([P, 1], F32, name=f"dot_inv{b}")
+            wed_inv = held.tile([P, 1], F32, name=f"wed_inv{b}")
+            nc.vector.tensor_tensor(dot_sum[:], dot_sum2[:, 0:1], dot_sum2[:, 1:2], ALU.add)
+            nc.vector.reciprocal(dot_inv[:], dot_sum[:])
+            nc.vector.reciprocal(wed_inv[:], wed_sum[:])
+            dot_term = held.tile([P, N], F32, name=f"dot_term{b}")
+            wed_term = held.tile([P, N], F32, name=f"wed_term{b}")
+            nc.vector.tensor_scalar(
+                dot_term[:], dot_exp[:], dot_inv[:], (1.0 - MIX) * N, ALU.mult, ALU.mult
+            )
+            nc.vector.tensor_scalar(wed_term[:], wed_exp[:], wed_inv[:], MIX * N, ALU.mult, ALU.mult)
+            nc.vector.tensor_tensor(
+                windows[b][:].indirect(offsets[:]), dot_term[:], wed_term[:], ALU.add
+            )
+            nc.sync.dma_start(out[b * P : (b + 1) * P, :], windows[b][:])

@@ -21,6 +21,10 @@ EPS = 1e-8
 FLOPS = 2 * C * N * E
 
 
+def half(h):
+    return slice(h * BANK, (h + 1) * BANK)
+
+
 def tile_dualpathgeomattention_kernel(tc, base, q, k, offs, out):
     nc = tc.nc
     with (
@@ -30,123 +34,133 @@ def tile_dualpathgeomattention_kernel(tc, base, q, k, offs, out):
         q_sb = held.tile([E, C], BF16, name="q_sb")
         k_sb = held.tile([E, N], BF16, name="k_sb")
         offsets = held.tile([P, N // 16], U16, name="offsets")
+        nc.scalar.dma_start(k_sb[:], k)
         nc.sync.dma_start(q_sb[:], q)
-        nc.sync.dma_start(k_sb[:], k)
         nc.sync.dma_start(offsets[:], offs)
-        windows = []
+        windows = [held.tile([P, S], F32, name=f"window{b}") for b in range(BLOCKS)]
         for b in range(BLOCKS):
-            window = held.tile([P, S], F32, name=f"window{b}")
-            nc.sync.dma_start(window[:], base[b * P : (b + 1) * P, :])
-            windows.append(window)
+            nc.sync.dma_start(windows[b][:], base[b * P : (b + 1) * P, :])
 
         ones = held.tile([E, P], BF16, name="ones")
-        nc.gpsimd.memset(ones[:], 1.0)
         eps_col = held.tile([P, 1], F32, name="eps_col")
+        minus_one = held.tile([P, 1], F32, name="minus_one")
+        nc.gpsimd.memset(ones[:], 1.0)
         nc.gpsimd.memset(eps_col[:], EPS)
+        nc.gpsimd.memset(minus_one[:], -1.0)
+
+        warm = held.tile([P, 1], F32, name="warm")
+        nc.scalar.activation(warm[:], eps_col[:], FUNC.Sqrt)
 
         q_sq = held.tile([E, C], BF16, name="q_sq")
         k_sq = held.tile([E, N], BF16, name="k_sq")
         nc.vector.tensor_tensor(q_sq[:], q_sb[:], q_sb[:], ALU.mult)
-        nc.vector.tensor_tensor(k_sq[:], k_sb[:], k_sb[:], ALU.mult)
+        for h in range(HALVES):
+            nc.vector.tensor_tensor(k_sq[:, half(h)], k_sb[:, half(h)], k_sb[:, half(h)], ALU.mult)
 
+        qn_ps = psum.tile([P, BLOCKS], F32, name="qn_ps")
+        kn_ps = [psum.tile([P, BANK], F32, name=f"kn_ps{h}") for h in range(HALVES)]
         dot_ps = [
             [psum.tile([P, BANK], F32, name=f"dot_ps{b}{h}") for h in range(HALVES)]
             for b in range(BLOCKS)
         ]
-        for b in range(BLOCKS):
+
+        def dot_products(b):
             for h in range(HALVES):
                 nc.tensor.matmul(
-                    dot_ps[b][h][:],
-                    q_sb[:, b * P : (b + 1) * P],
-                    k_sb[:, h * BANK : (h + 1) * BANK],
-                    start=True,
-                    stop=True,
+                    dot_ps[b][h][:], q_sb[:, b * P : (b + 1) * P], k_sb[:, half(h)], start=True, stop=True
                 )
-        qn_ps = psum.tile([P, BLOCKS], F32, name="qn_ps")
+
+        dot_products(0)
         for b in range(BLOCKS):
             nc.tensor.matmul(
                 qn_ps[:, b : b + 1], q_sq[:, b * P : (b + 1) * P], ones[:, 0:1], start=True, stop=True
             )
+        for h in range(HALVES):
+            nc.tensor.matmul(kn_ps[h][:], ones[:], k_sq[:, half(h)], start=True, stop=True)
+        dot_products(1)
         qn = held.tile([P, BLOCKS], F32, name="qn")
         nc.vector.tensor_copy(qn[:], qn_ps[:])
-        kn_ps = [psum.tile([P, BANK], F32, name=f"kn_ps{h}") for h in range(HALVES)]
-        for h in range(HALVES):
-            nc.tensor.matmul(
-                kn_ps[h][:], ones[:], k_sq[:, h * BANK : (h + 1) * BANK], start=True, stop=True
-            )
 
         dot_sq = [held.tile([P, N], F32, name=f"dot_sq{b}") for b in range(BLOCKS)]
         for b in range(BLOCKS):
             for h in range(HALVES):
-                cols = slice(h * BANK, (h + 1) * BANK)
-                nc.scalar.activation(dot_sq[b][:, cols], dot_ps[b][h][:], FUNC.Square)
+                nc.scalar.activation(dot_sq[b][:, half(h)], dot_ps[b][h][:], FUNC.Square)
 
-        wed = []
-        wed_shift = []
-        for b in range(BLOCKS):
+        clamped = [held.tile([P, N], F32, name=f"clamped{b}") for b in range(BLOCKS)]
+        clamped_top = [held.tile([P, 1], F32, name=f"clamped_top{b}") for b in range(BLOCKS)]
+        dot_shift = [held.tile([P, 1], F32, name=f"dot_shift{b}") for b in range(BLOCKS)]
+        wed = [held.tile([P, N], F32, name=f"wed{b}") for b in range(BLOCKS)]
+        wed_shift = [held.tile([P, 1], F32, name=f"wed_shift{b}") for b in range(BLOCKS)]
+
+        def clamped_gram(b):
             gram = held.tile([P, N], F32, name=f"gram{b}")
-            clamped = held.tile([P, N], F32, name=f"clamped{b}")
-            clamped_top = held.tile([P, HALVES], F32, name=f"clamped_top{b}")
-            wed_b = held.tile([P, N], F32, name=f"wed{b}")
+            top2 = held.tile([P, HALVES], F32, name=f"clamped_top2{b}")
             for h in range(HALVES):
-                cols = slice(h * BANK, (h + 1) * BANK)
                 nc.vector.scalar_tensor_tensor(
-                    gram[:, cols], kn_ps[h][:], qn[:, b : b + 1], dot_sq[b][:, cols], ALU.mult, ALU.subtract
+                    gram[:, half(h)], kn_ps[h][:], qn[:, b : b + 1], dot_sq[b][:, half(h)], ALU.mult, ALU.subtract
                 )
             for h in range(HALVES):
-                cols = slice(h * BANK, (h + 1) * BANK)
                 nc.vector.tensor_scalar(
-                    clamped[:, cols], gram[:, cols], 0.0, None, ALU.max, ALU.max,
-                    accum_out=clamped_top[:, h : h + 1],
+                    clamped[b][:, half(h)], gram[:, half(h)], 0.0, None, ALU.max, ALU.max,
+                    accum_out=top2[:, h : h + 1],
                 )
-                nc.scalar.activation(wed_b[:, cols], clamped[:, cols], FUNC.Sqrt, bias=eps_col[:])
-            row_top = held.tile([P, 1], F32, name=f"row_top{b}")
+            nc.vector.tensor_tensor(clamped_top[b][:], top2[:, 0:1], top2[:, 1:2], ALU.max)
+
+        def dot_maximum(b):
+            top2 = held.tile([P, HALVES], F32, name=f"dot_top2{b}")
+            for h in range(HALVES):
+                nc.vector.reduce_max(top2[:, h : h + 1], dot_ps[b][h][:], axis=AXIS.X)
+            nc.vector.tensor_scalar(dot_shift[b][:], top2[:, 0:1], top2[:, 1:2], -SC, ALU.max, ALU.mult)
+
+        def roots(b):
+            for h in range(HALVES):
+                nc.scalar.activation(wed[b][:, half(h)], clamped[b][:, half(h)], FUNC.Sqrt, bias=eps_col[:])
             wed_top = held.tile([P, 1], F32, name=f"wed_top{b}")
-            shift = held.tile([P, 1], F32, name=f"wed_shift{b}")
-            nc.vector.tensor_tensor(row_top[:], clamped_top[:, 0:1], clamped_top[:, 1:2], ALU.max)
-            nc.scalar.activation(wed_top[:], row_top[:], FUNC.Sqrt, bias=eps_col[:])
-            nc.vector.tensor_scalar_mul(shift[:], wed_top[:], -SC)
-            wed.append(wed_b)
-            wed_shift.append(shift)
+            nc.scalar.activation(wed_top[:], clamped_top[b][:], FUNC.Sqrt, bias=eps_col[:])
+            nc.scalar.mul(wed_shift[b][:], wed_top[:], -SC)
 
-        dot_shift = []
-        for b in range(BLOCKS):
-            dot_top = held.tile([P, HALVES], F32, name=f"dot_top{b}")
-            shift = held.tile([P, 1], F32, name=f"dot_shift{b}")
-            for h in range(HALVES):
-                nc.vector.reduce_max(dot_top[:, h : h + 1], dot_ps[b][h][:], axis=AXIS.X)
-            nc.vector.tensor_scalar(
-                shift[:], dot_top[:, 0:1], dot_top[:, 1:2], -SC, ALU.max, ALU.mult
-            )
-            dot_shift.append(shift)
+        dot_term = [held.tile([P, N], F32, name=f"dot_term{b}") for b in range(BLOCKS)]
+        wed_term = [held.tile([P, N], F32, name=f"wed_term{b}") for b in range(BLOCKS)]
 
-        for b in range(BLOCKS):
+        def dot_softmax(b):
             dot_exp = held.tile([P, N], F32, name=f"dot_exp{b}")
-            wed_exp = held.tile([P, N], F32, name=f"wed_exp{b}")
-            dot_sum2 = held.tile([P, HALVES], F32, name=f"dot_sum2{b}")
+            sum2 = held.tile([P, HALVES], F32, name=f"dot_sum2{b}")
             dot_sum = held.tile([P, 1], F32, name=f"dot_sum{b}")
-            wed_sum = held.tile([P, 1], F32, name=f"wed_sum{b}")
+            dot_inv = held.tile([P, 1], F32, name=f"dot_inv{b}")
             for h in range(HALVES):
-                cols = slice(h * BANK, (h + 1) * BANK)
                 nc.scalar.activation(
-                    dot_exp[:, cols], dot_ps[b][h][:], FUNC.Exp, bias=dot_shift[b][:], scale=SC,
-                    accum_out=dot_sum2[:, h : h + 1],
+                    dot_exp[:, half(h)], dot_ps[b][h][:], FUNC.Exp, bias=dot_shift[b][:], scale=SC,
+                    accum_out=sum2[:, h : h + 1],
                 )
+            nc.gpsimd.tensor_tensor(dot_sum[:], sum2[:, 0:1], sum2[:, 1:2], ALU.add)
+            nc.gpsimd.tensor_tensor(dot_inv[:], dot_sum[:], minus_one[:], ALU.pow)
+            nc.gpsimd.tensor_scalar(dot_term[b][:], dot_exp[:], dot_inv[:], (1.0 - MIX) * N, ALU.mult, ALU.mult)
+
+        def wed_softmax(b):
+            wed_exp = held.tile([P, N], F32, name=f"wed_exp{b}")
+            wed_sum = held.tile([P, 1], F32, name=f"wed_sum{b}")
+            wed_inv = held.tile([P, 1], F32, name=f"wed_inv{b}")
             nc.scalar.activation(
                 wed_exp[:], wed[b][:], FUNC.Exp, bias=wed_shift[b][:], scale=SC, accum_out=wed_sum[:]
             )
-            dot_inv = held.tile([P, 1], F32, name=f"dot_inv{b}")
-            wed_inv = held.tile([P, 1], F32, name=f"wed_inv{b}")
-            nc.vector.tensor_tensor(dot_sum[:], dot_sum2[:, 0:1], dot_sum2[:, 1:2], ALU.add)
-            nc.vector.reciprocal(dot_inv[:], dot_sum[:])
             nc.vector.reciprocal(wed_inv[:], wed_sum[:])
-            dot_term = held.tile([P, N], F32, name=f"dot_term{b}")
-            wed_term = held.tile([P, N], F32, name=f"wed_term{b}")
-            nc.vector.tensor_scalar(
-                dot_term[:], dot_exp[:], dot_inv[:], (1.0 - MIX) * N, ALU.mult, ALU.mult
-            )
-            nc.vector.tensor_scalar(wed_term[:], wed_exp[:], wed_inv[:], MIX * N, ALU.mult, ALU.mult)
+            nc.vector.tensor_scalar(wed_term[b][:], wed_exp[:], wed_inv[:], MIX * N, ALU.mult, ALU.mult)
+
+        def place(b):
             nc.vector.tensor_tensor(
-                windows[b][:].indirect(offsets[:]), dot_term[:], wed_term[:], ALU.add
+                windows[b][:].indirect(offsets[:]), dot_term[b][:], wed_term[b][:], ALU.add
             )
             nc.sync.dma_start(out[b * P : (b + 1) * P, :], windows[b][:])
+
+        clamped_gram(0)
+        roots(0)
+        dot_maximum(0)
+        clamped_gram(1)
+        dot_maximum(1)
+        dot_softmax(0)
+        wed_softmax(0)
+        place(0)
+        dot_softmax(1)
+        roots(1)
+        wed_softmax(1)
+        place(1)

@@ -42,14 +42,14 @@ def tile_dualpathgeomattention_kernel(tc, base, q, k, offs, out):
             nc.sync.dma_start(windows[b][:], base[b * P : (b + 1) * P, :])
 
         ones = held.tile([E, P], BF16, name="ones")
-        eps_col = held.tile([P, 1], F32, name="eps_col")
+        scaled_eps = held.tile([P, 1], F32, name="scaled_eps")
         minus_one = held.tile([P, 1], F32, name="minus_one")
         nc.gpsimd.memset(ones[:], 1.0)
-        nc.gpsimd.memset(eps_col[:], EPS)
+        nc.gpsimd.memset(scaled_eps[:], SC * SC * EPS)
         nc.gpsimd.memset(minus_one[:], -1.0)
 
         warm = held.tile([P, 1], F32, name="warm")
-        nc.scalar.activation(warm[:], eps_col[:], FUNC.Sqrt)
+        nc.scalar.activation(warm[:], scaled_eps[:], FUNC.Sqrt)
 
         q_sq = held.tile([E, C], BF16, name="q_sq")
         k_sq = held.tile([E, N], BF16, name="k_sq")
@@ -86,81 +86,50 @@ def tile_dualpathgeomattention_kernel(tc, base, q, k, offs, out):
             for h in range(HALVES):
                 nc.scalar.activation(dot_sq[b][:, half(h)], dot_ps[b][h][:], FUNC.Square)
 
-        clamped = [held.tile([P, N], F32, name=f"clamped{b}") for b in range(BLOCKS)]
-        clamped_top = [held.tile([P, 1], F32, name=f"clamped_top{b}") for b in range(BLOCKS)]
-        dot_shift = [held.tile([P, 1], F32, name=f"dot_shift{b}") for b in range(BLOCKS)]
-        wed = [held.tile([P, N], F32, name=f"wed{b}") for b in range(BLOCKS)]
-        wed_shift = [held.tile([P, 1], F32, name=f"wed_shift{b}") for b in range(BLOCKS)]
-
-        def clamped_gram(b):
+        wed_score = [held.tile([P, N], F32, name=f"wed_score{b}") for b in range(BLOCKS)]
+        for b in range(BLOCKS):
             gram = held.tile([P, N], F32, name=f"gram{b}")
-            top2 = held.tile([P, HALVES], F32, name=f"clamped_top2{b}")
+            clamped = held.tile([P, N], F32, name=f"clamped{b}")
             for h in range(HALVES):
                 nc.vector.scalar_tensor_tensor(
                     gram[:, half(h)], kn_ps[h][:], qn[:, b : b + 1], dot_sq[b][:, half(h)], ALU.mult, ALU.subtract
                 )
             for h in range(HALVES):
-                nc.vector.tensor_scalar(
-                    clamped[b][:, half(h)], gram[:, half(h)], 0.0, None, ALU.max, ALU.max,
-                    accum_out=top2[:, h : h + 1],
+                nc.vector.tensor_scalar_max(clamped[:, half(h)], gram[:, half(h)], 0.0)
+                nc.scalar.activation(
+                    wed_score[b][:, half(h)], clamped[:, half(h)], FUNC.Sqrt, bias=scaled_eps[:], scale=SC * SC
                 )
-            nc.vector.tensor_tensor(clamped_top[b][:], top2[:, 0:1], top2[:, 1:2], ALU.max)
 
-        def dot_maximum(b):
-            top2 = held.tile([P, HALVES], F32, name=f"dot_top2{b}")
+        dot_shift = [held.tile([P, 1], F32, name=f"dot_shift{b}") for b in range(BLOCKS)]
+        wed_shift = [held.tile([P, 1], F32, name=f"wed_shift{b}") for b in range(BLOCKS)]
+        for b in range(BLOCKS):
+            dot_top2 = held.tile([P, HALVES], F32, name=f"dot_top2{b}")
             for h in range(HALVES):
-                nc.vector.reduce_max(top2[:, h : h + 1], dot_ps[b][h][:], axis=AXIS.X)
-            nc.vector.tensor_scalar(dot_shift[b][:], top2[:, 0:1], top2[:, 1:2], -SC, ALU.max, ALU.mult)
+                nc.vector.reduce_max(dot_top2[:, h : h + 1], dot_ps[b][h][:], axis=AXIS.X)
+            nc.vector.tensor_scalar(dot_shift[b][:], dot_top2[:, 0:1], dot_top2[:, 1:2], -SC, ALU.max, ALU.mult)
+            nc.vector.reduce_max(wed_shift[b][:], wed_score[b][:], axis=AXIS.X, negate=True)
 
-        def roots(b):
-            for h in range(HALVES):
-                nc.scalar.activation(wed[b][:, half(h)], clamped[b][:, half(h)], FUNC.Sqrt, bias=eps_col[:])
-            wed_top = held.tile([P, 1], F32, name=f"wed_top{b}")
-            nc.scalar.activation(wed_top[:], clamped_top[b][:], FUNC.Sqrt, bias=eps_col[:])
-            nc.scalar.mul(wed_shift[b][:], wed_top[:], -SC)
+        def term_of(name, exps, total, gain, multiplier):
+            inverse = held.tile([P, 1], F32, name=f"{name}_inverse")
+            term = held.tile([P, N], F32, name=f"{name}_term")
+            nc.gpsimd.tensor_tensor(inverse[:], total[:], minus_one[:], ALU.pow)
+            multiplier.tensor_scalar(term[:], exps[:], inverse[:], gain, ALU.mult, ALU.mult)
+            return term
 
-        dot_term = [held.tile([P, N], F32, name=f"dot_term{b}") for b in range(BLOCKS)]
-        wed_term = [held.tile([P, N], F32, name=f"wed_term{b}") for b in range(BLOCKS)]
-
-        def dot_softmax(b):
+        for b in range(BLOCKS):
             dot_exp = held.tile([P, N], F32, name=f"dot_exp{b}")
-            sum2 = held.tile([P, HALVES], F32, name=f"dot_sum2{b}")
+            wed_exp = held.tile([P, N], F32, name=f"wed_exp{b}")
+            dot_sum2 = held.tile([P, HALVES], F32, name=f"dot_sum2{b}")
             dot_sum = held.tile([P, 1], F32, name=f"dot_sum{b}")
-            dot_inv = held.tile([P, 1], F32, name=f"dot_inv{b}")
+            wed_sum = held.tile([P, 1], F32, name=f"wed_sum{b}")
             for h in range(HALVES):
                 nc.scalar.activation(
                     dot_exp[:, half(h)], dot_ps[b][h][:], FUNC.Exp, bias=dot_shift[b][:], scale=SC,
-                    accum_out=sum2[:, h : h + 1],
+                    accum_out=dot_sum2[:, h : h + 1],
                 )
-            nc.gpsimd.tensor_tensor(dot_sum[:], sum2[:, 0:1], sum2[:, 1:2], ALU.add)
-            nc.gpsimd.tensor_tensor(dot_inv[:], dot_sum[:], minus_one[:], ALU.pow)
-            nc.gpsimd.tensor_scalar(dot_term[b][:], dot_exp[:], dot_inv[:], (1.0 - MIX) * N, ALU.mult, ALU.mult)
-
-        def wed_softmax(b):
-            wed_exp = held.tile([P, N], F32, name=f"wed_exp{b}")
-            wed_sum = held.tile([P, 1], F32, name=f"wed_sum{b}")
-            wed_inv = held.tile([P, 1], F32, name=f"wed_inv{b}")
-            nc.scalar.activation(
-                wed_exp[:], wed[b][:], FUNC.Exp, bias=wed_shift[b][:], scale=SC, accum_out=wed_sum[:]
-            )
-            nc.vector.reciprocal(wed_inv[:], wed_sum[:])
-            nc.vector.tensor_scalar(wed_term[b][:], wed_exp[:], wed_inv[:], MIX * N, ALU.mult, ALU.mult)
-
-        def place(b):
-            nc.vector.tensor_tensor(
-                windows[b][:].indirect(offsets[:]), dot_term[b][:], wed_term[b][:], ALU.add
-            )
+            nc.scalar.activation(wed_exp[:], wed_score[b][:], FUNC.Exp, bias=wed_shift[b][:], accum_out=wed_sum[:])
+            nc.gpsimd.tensor_tensor(dot_sum[:], dot_sum2[:, 0:1], dot_sum2[:, 1:2], ALU.add)
+            dot_term = term_of(f"dot{b}", dot_exp, dot_sum, (1.0 - MIX) * N, nc.gpsimd)
+            wed_term = term_of(f"wed{b}", wed_exp, wed_sum, MIX * N, nc.vector if b == 0 else nc.gpsimd)
+            nc.vector.tensor_tensor(windows[b][:].indirect(offsets[:]), dot_term[:], wed_term[:], ALU.add)
             nc.sync.dma_start(out[b * P : (b + 1) * P, :], windows[b][:])
-
-        clamped_gram(0)
-        roots(0)
-        dot_maximum(0)
-        clamped_gram(1)
-        dot_maximum(1)
-        dot_softmax(0)
-        wed_softmax(0)
-        place(0)
-        dot_softmax(1)
-        roots(1)
-        wed_softmax(1)
-        place(1)

@@ -43,10 +43,8 @@ def tile_dualpathgeomattention_kernel(tc, base, q, k, offs, out):
 
         ones = held.tile([E, P], BF16, name="ones")
         scaled_eps = held.tile([P, 1], F32, name="scaled_eps")
-        minus_one = held.tile([P, 1], F32, name="minus_one")
         nc.gpsimd.memset(ones[:], 1.0)
         nc.gpsimd.memset(scaled_eps[:], SC * SC * EPS)
-        nc.gpsimd.memset(minus_one[:], -1.0)
 
         warm = held.tile([P, 1], F32, name="warm")
         nc.scalar.activation(warm[:], scaled_eps[:], FUNC.Sqrt)
@@ -109,27 +107,37 @@ def tile_dualpathgeomattention_kernel(tc, base, q, k, offs, out):
             nc.vector.tensor_scalar(dot_shift[b][:], dot_top2[:, 0:1], dot_top2[:, 1:2], -SC, ALU.max, ALU.mult)
             nc.vector.reduce_max(wed_shift[b][:], wed_score[b][:], axis=AXIS.X, negate=True)
 
-        def term_of(name, exps, total, gain, multiplier):
-            inverse = held.tile([P, 1], F32, name=f"{name}_inverse")
-            term = held.tile([P, N], F32, name=f"{name}_term")
-            nc.gpsimd.tensor_tensor(inverse[:], total[:], minus_one[:], ALU.pow)
-            multiplier.tensor_scalar(term[:], exps[:], inverse[:], gain, ALU.mult, ALU.mult)
-            return term
-
+        dot_exp = [held.tile([P, N], F32, name=f"dot_exp{b}") for b in range(BLOCKS)]
+        wed_exp = [held.tile([P, N], F32, name=f"wed_exp{b}") for b in range(BLOCKS)]
+        dot_sum2 = [held.tile([P, HALVES], F32, name=f"dot_sum2{b}") for b in range(BLOCKS)]
+        wed_sum2 = [held.tile([P, HALVES], F32, name=f"wed_sum2{b}") for b in range(BLOCKS)]
         for b in range(BLOCKS):
-            dot_exp = held.tile([P, N], F32, name=f"dot_exp{b}")
-            wed_exp = held.tile([P, N], F32, name=f"wed_exp{b}")
-            dot_sum2 = held.tile([P, HALVES], F32, name=f"dot_sum2{b}")
-            dot_sum = held.tile([P, 1], F32, name=f"dot_sum{b}")
-            wed_sum = held.tile([P, 1], F32, name=f"wed_sum{b}")
             for h in range(HALVES):
                 nc.scalar.activation(
-                    dot_exp[:, half(h)], dot_ps[b][h][:], FUNC.Exp, bias=dot_shift[b][:], scale=SC,
-                    accum_out=dot_sum2[:, h : h + 1],
+                    dot_exp[b][:, half(h)], dot_ps[b][h][:], FUNC.Exp, bias=dot_shift[b][:], scale=SC,
+                    accum_out=dot_sum2[b][:, h : h + 1],
                 )
-            nc.scalar.activation(wed_exp[:], wed_score[b][:], FUNC.Exp, bias=wed_shift[b][:], accum_out=wed_sum[:])
-            nc.gpsimd.tensor_tensor(dot_sum[:], dot_sum2[:, 0:1], dot_sum2[:, 1:2], ALU.add)
-            dot_term = term_of(f"dot{b}", dot_exp, dot_sum, (1.0 - MIX) * N, nc.gpsimd)
-            wed_term = term_of(f"wed{b}", wed_exp, wed_sum, MIX * N, nc.vector if b == 0 else nc.gpsimd)
-            nc.vector.tensor_tensor(windows[b][:].indirect(offsets[:]), dot_term[:], wed_term[:], ALU.add)
+            for h in range(HALVES):
+                nc.scalar.activation(
+                    wed_exp[b][:, half(h)], wed_score[b][:, half(h)], FUNC.Exp, bias=wed_shift[b][:],
+                    accum_out=wed_sum2[b][:, h : h + 1],
+                )
+
+        def term_of(name, b, exps, sum2, gain):
+            shrunk = held.tile([P, 1], F32, name=f"{name}_shrunk{b}")
+            weight = held.tile([P, 1], F32, name=f"{name}_weight{b}")
+            term = held.tile([P, N], F32, name=f"{name}_term{b}")
+            nc.vector.tensor_scalar(shrunk[:], sum2[:, 0:1], sum2[:, 1:2], 1.0 / gain, ALU.add, ALU.mult)
+            nc.vector.reciprocal(weight[:], shrunk[:])
+            if b == 0:
+                nc.vector.tensor_scalar_mul(term[:], exps[:], weight[:])
+            else:
+                nc.scalar.activation(term[:], exps[:], FUNC.Copy, scale=weight[:])
+            return term
+
+        dot_term = [term_of("dot", b, dot_exp[b], dot_sum2[b], (1.0 - MIX) * N) for b in range(BLOCKS)]
+        wed_term = [term_of("wed", b, wed_exp[b], wed_sum2[b], MIX * N) for b in range(BLOCKS)]
+
+        for b in range(BLOCKS):
+            nc.vector.tensor_tensor(windows[b][:].indirect(offsets[:]), dot_term[b][:], wed_term[b][:], ALU.add)
             nc.sync.dma_start(out[b * P : (b + 1) * P, :], windows[b][:])

@@ -19,6 +19,7 @@ MIX = 1.0 / (1.0 + math.exp(-1.0))
 EPS = 1e-8
 
 FLOPS = 2 * C * N * E
+WARM_MATMULS = 4
 
 
 def half(h):
@@ -41,13 +42,16 @@ def tile_dualpathgeomattention_kernel(tc, base, q, k, offs, out):
         for b in range(BLOCKS):
             nc.sync.dma_start(windows[b][:], base[b * P : (b + 1) * P, :])
 
-        ones = held.tile([E, P], BF16, name="ones")
+        ones = held.tile([E, BANK], BF16, name="ones")
         scaled_eps = held.tile([P, 1], F32, name="scaled_eps")
         nc.gpsimd.memset(ones[:], 1.0)
         nc.gpsimd.memset(scaled_eps[:], SC * SC * EPS)
 
         warm = held.tile([P, 1], F32, name="warm")
         nc.scalar.activation(warm[:], scaled_eps[:], FUNC.Sqrt)
+        warm_ps = psum.tile([P, BANK], F32, name="warm_ps")
+        for i in range(WARM_MATMULS):
+            nc.tensor.matmul(warm_ps[:], ones[:, 0:P], ones[:], start=True, stop=True)
 
         q_sq = held.tile([E, C], BF16, name="q_sq")
         k_sq = held.tile([E, N], BF16, name="k_sq")
@@ -62,20 +66,20 @@ def tile_dualpathgeomattention_kernel(tc, base, q, k, offs, out):
             for b in range(BLOCKS)
         ]
 
-        def dot_products(b):
-            for h in range(HALVES):
-                nc.tensor.matmul(
-                    dot_ps[b][h][:], q_sb[:, b * P : (b + 1) * P], k_sb[:, half(h)], start=True, stop=True
-                )
+        def dot_product(b, h):
+            nc.tensor.matmul(
+                dot_ps[b][h][:], q_sb[:, b * P : (b + 1) * P], k_sb[:, half(h)], start=True, stop=True
+            )
 
-        dot_products(0)
         for b in range(BLOCKS):
             nc.tensor.matmul(
                 qn_ps[:, b : b + 1], q_sq[:, b * P : (b + 1) * P], ones[:, 0:1], start=True, stop=True
             )
         for h in range(HALVES):
-            nc.tensor.matmul(kn_ps[h][:], ones[:], k_sq[:, half(h)], start=True, stop=True)
-        dot_products(1)
+            dot_product(0, h)
+            nc.tensor.matmul(kn_ps[h][:], ones[:, 0:P], k_sq[:, half(h)], start=True, stop=True)
+        for h in range(HALVES):
+            dot_product(1, h)
         qn = held.tile([P, BLOCKS], F32, name="qn")
         nc.vector.tensor_copy(qn[:], qn_ps[:])
 
@@ -84,60 +88,71 @@ def tile_dualpathgeomattention_kernel(tc, base, q, k, offs, out):
             for h in range(HALVES):
                 nc.scalar.activation(dot_sq[b][:, half(h)], dot_ps[b][h][:], FUNC.Square)
 
+        clamped = [held.tile([P, N], F32, name=f"clamped{b}") for b in range(BLOCKS)]
+        tops = [held.tile([P, 2], F32, name=f"tops{b}") for b in range(BLOCKS)]
+        dot_shift = [held.tile([P, 1], F32, name=f"dot_shift{b}") for b in range(BLOCKS)]
+        wed_shift = [held.tile([P, 1], F32, name=f"wed_shift{b}") for b in range(BLOCKS)]
         wed_score = [held.tile([P, N], F32, name=f"wed_score{b}") for b in range(BLOCKS)]
-        for b in range(BLOCKS):
+
+        def vector_share(b):
             gram = held.tile([P, N], F32, name=f"gram{b}")
-            clamped = held.tile([P, N], F32, name=f"clamped{b}")
+            tops_by_half = held.tile([P, 2 * HALVES], F32, name=f"tops_by_half{b}")
+            for h in range(HALVES):
+                nc.vector.reduce_max(tops_by_half[:, h : h + 1], dot_ps[b][h][:], axis=AXIS.X)
             for h in range(HALVES):
                 nc.vector.scalar_tensor_tensor(
                     gram[:, half(h)], kn_ps[h][:], qn[:, b : b + 1], dot_sq[b][:, half(h)], ALU.mult, ALU.subtract
                 )
             for h in range(HALVES):
-                nc.vector.tensor_scalar_max(clamped[:, half(h)], gram[:, half(h)], 0.0)
-                nc.scalar.activation(
-                    wed_score[b][:, half(h)], clamped[:, half(h)], FUNC.Sqrt, bias=scaled_eps[:], scale=SC * SC
+                nc.vector.tensor_scalar(
+                    clamped[b][:, half(h)], gram[:, half(h)], 0.0, None, ALU.max, ALU.max,
+                    accum_out=tops_by_half[:, HALVES + h : HALVES + h + 1],
                 )
+            nc.vector.reduce_max(tops[b][:], tops_by_half[:].rearrange("p (t h) -> p t h", h=HALVES), axis=AXIS.X)
+            nc.vector.tensor_scalar_mul(dot_shift[b][:], tops[b][:, 0:1], -SC)
 
-        dot_shift = [held.tile([P, 1], F32, name=f"dot_shift{b}") for b in range(BLOCKS)]
-        wed_shift = [held.tile([P, 1], F32, name=f"wed_shift{b}") for b in range(BLOCKS)]
-        for b in range(BLOCKS):
-            dot_top2 = held.tile([P, HALVES], F32, name=f"dot_top2{b}")
-            for h in range(HALVES):
-                nc.vector.reduce_max(dot_top2[:, h : h + 1], dot_ps[b][h][:], axis=AXIS.X)
-            nc.vector.tensor_scalar(dot_shift[b][:], dot_top2[:, 0:1], dot_top2[:, 1:2], -SC, ALU.max, ALU.mult)
-            nc.vector.reduce_max(wed_shift[b][:], wed_score[b][:], axis=AXIS.X, negate=True)
-
-        dot_exp = [held.tile([P, N], F32, name=f"dot_exp{b}") for b in range(BLOCKS)]
-        wed_exp = [held.tile([P, N], F32, name=f"wed_exp{b}") for b in range(BLOCKS)]
-        dot_sum2 = [held.tile([P, HALVES], F32, name=f"dot_sum2{b}") for b in range(BLOCKS)]
-        wed_sum2 = [held.tile([P, HALVES], F32, name=f"wed_sum2{b}") for b in range(BLOCKS)]
-        for b in range(BLOCKS):
+        def roots(b):
             for h in range(HALVES):
                 nc.scalar.activation(
-                    dot_exp[b][:, half(h)], dot_ps[b][h][:], FUNC.Exp, bias=dot_shift[b][:], scale=SC,
-                    accum_out=dot_sum2[b][:, h : h + 1],
+                    wed_score[b][:, half(h)], clamped[b][:, half(h)], FUNC.Sqrt, bias=scaled_eps[:], scale=SC * SC
                 )
-            for h in range(HALVES):
-                nc.scalar.activation(
-                    wed_exp[b][:, half(h)], wed_score[b][:, half(h)], FUNC.Exp, bias=wed_shift[b][:],
-                    accum_out=wed_sum2[b][:, h : h + 1],
-                )
+            wed_top = held.tile([P, 1], F32, name=f"wed_top{b}")
+            nc.scalar.activation(wed_top[:], tops[b][:, 1:2], FUNC.Sqrt, bias=scaled_eps[:], scale=SC * SC)
+            nc.scalar.mul(wed_shift[b][:], wed_top[:], -1.0)
 
-        def term_of(name, b, exps, sum2, gain):
-            shrunk = held.tile([P, 1], F32, name=f"{name}_shrunk{b}")
-            weight = held.tile([P, 1], F32, name=f"{name}_weight{b}")
-            term = held.tile([P, N], F32, name=f"{name}_term{b}")
-            nc.vector.tensor_scalar(shrunk[:], sum2[:, 0:1], sum2[:, 1:2], 1.0 / gain, ALU.add, ALU.mult)
-            nc.vector.reciprocal(weight[:], shrunk[:])
-            if b == 0:
-                nc.vector.tensor_scalar_mul(term[:], exps[:], weight[:])
-            else:
-                nc.scalar.activation(term[:], exps[:], FUNC.Copy, scale=weight[:])
+        def term_of(name, exps, row_sum, gain):
+            inverse = held.tile([P, 1], F32, name=f"{name}_inverse")
+            term = held.tile([P, N], F32, name=f"{name}_term")
+            nc.vector.reciprocal(inverse[:], row_sum[:])
+            nc.vector.tensor_scalar(term[:], exps[:], inverse[:], gain, ALU.mult, ALU.mult)
             return term
 
-        dot_term = [term_of("dot", b, dot_exp[b], dot_sum2[b], (1.0 - MIX) * N) for b in range(BLOCKS)]
-        wed_term = [term_of("wed", b, wed_exp[b], wed_sum2[b], MIX * N) for b in range(BLOCKS)]
+        def softmax_terms(b):
+            dot_exp = held.tile([P, N], F32, name=f"dot_exp{b}")
+            wed_exp = held.tile([P, N], F32, name=f"wed_exp{b}")
+            dot_sum_by_half = held.tile([P, HALVES], F32, name=f"dot_sum_by_half{b}")
+            dot_sum = held.tile([P, 1], F32, name=f"dot_sum{b}")
+            wed_sum = held.tile([P, 1], F32, name=f"wed_sum{b}")
+            for h in range(HALVES):
+                nc.scalar.activation(
+                    dot_exp[:, half(h)], dot_ps[b][h][:], FUNC.Exp, bias=dot_shift[b][:], scale=SC,
+                    accum_out=dot_sum_by_half[:, h : h + 1],
+                )
+            nc.scalar.activation(wed_exp[:], wed_score[b][:], FUNC.Exp, bias=wed_shift[b][:], accum_out=wed_sum[:])
+            nc.vector.tensor_tensor(dot_sum[:], dot_sum_by_half[:, 0:1], dot_sum_by_half[:, 1:2], ALU.add)
+            dot_term = term_of(f"dot{b}", dot_exp, dot_sum, (1.0 - MIX) * N)
+            wed_term = term_of(f"wed{b}", wed_exp, wed_sum, MIX * N)
+            return dot_term, wed_term
 
-        for b in range(BLOCKS):
-            nc.vector.tensor_tensor(windows[b][:].indirect(offsets[:]), dot_term[b][:], wed_term[b][:], ALU.add)
+        def place(b, dot_term, wed_term):
+            nc.vector.tensor_tensor(windows[b][:].indirect(offsets[:]), dot_term[:], wed_term[:], ALU.add)
             nc.sync.dma_start(out[b * P : (b + 1) * P, :], windows[b][:])
+
+        vector_share(0)
+        roots(0)
+        terms0 = softmax_terms(0)
+        vector_share(1)
+        place(0, *terms0)
+        roots(1)
+        terms1 = softmax_terms(1)
+        place(1, *terms1)

@@ -46,6 +46,8 @@ def tile_dualpathgeomattention_kernel(tc, base, q, k, offs, out):
         scaled_eps = held.tile([P, 1], F32, name="scaled_eps")
         nc.gpsimd.memset(ones[:], 1.0)
         nc.gpsimd.memset(scaled_eps[:], SC * SC * EPS)
+        minus_one = held.tile([P, 1], F32, name="minus_one")
+        nc.gpsimd.memset(minus_one[:], -1.0)
 
         warm = held.tile([P, 1], F32, name="warm")
         nc.scalar.activation(warm[:], scaled_eps[:], FUNC.Sqrt)
@@ -98,8 +100,6 @@ def tile_dualpathgeomattention_kernel(tc, base, q, k, offs, out):
             gram = held.tile([P, N], F32, name=f"gram{b}")
             tops_by_half = held.tile([P, 2 * HALVES], F32, name=f"tops_by_half{b}")
             for h in range(HALVES):
-                nc.vector.reduce_max(tops_by_half[:, h : h + 1], dot_ps[b][h][:], axis=AXIS.X)
-            for h in range(HALVES):
                 nc.vector.scalar_tensor_tensor(
                     gram[:, half(h)], kn_ps[h][:], qn[:, b : b + 1], dot_sq[b][:, half(h)], ALU.mult, ALU.subtract
                 )
@@ -108,6 +108,8 @@ def tile_dualpathgeomattention_kernel(tc, base, q, k, offs, out):
                     clamped[b][:, half(h)], gram[:, half(h)], 0.0, None, ALU.max, ALU.max,
                     accum_out=tops_by_half[:, HALVES + h : HALVES + h + 1],
                 )
+            for h in range(HALVES):
+                nc.vector.reduce_max(tops_by_half[:, h : h + 1], dot_ps[b][h][:], axis=AXIS.X)
             nc.vector.reduce_max(tops[b][:], tops_by_half[:].rearrange("p (t h) -> p t h", h=HALVES), axis=AXIS.X)
             nc.vector.tensor_scalar_mul(dot_shift[b][:], tops[b][:, 0:1], -SC)
 
@@ -120,28 +122,41 @@ def tile_dualpathgeomattention_kernel(tc, base, q, k, offs, out):
             nc.scalar.activation(wed_top[:], tops[b][:, 1:2], FUNC.Sqrt, bias=scaled_eps[:], scale=SC * SC)
             nc.scalar.mul(wed_shift[b][:], wed_top[:], -1.0)
 
-        def term_of(name, exps, row_sum, gain):
-            inverse = held.tile([P, 1], F32, name=f"{name}_inverse")
-            term = held.tile([P, N], F32, name=f"{name}_term")
-            nc.vector.reciprocal(inverse[:], row_sum[:])
-            nc.vector.tensor_scalar(term[:], exps[:], inverse[:], gain, ALU.mult, ALU.mult)
-            return term
+        def weight_of(name, b, sum_by_half, gain):
+            shrunk = held.tile([P, 1], F32, name=f"{name}_shrunk{b}")
+            weight = held.tile([P, 1], F32, name=f"{name}_weight{b}")
+            engine = nc.vector if b == 0 else nc.gpsimd
+            engine.tensor_scalar(shrunk[:], sum_by_half[:, 0:1], sum_by_half[:, 1:2], 1.0 / gain, ALU.add, ALU.mult)
+            if b == 0:
+                nc.vector.reciprocal(weight[:], shrunk[:])
+            else:
+                nc.gpsimd.tensor_tensor(weight[:], shrunk[:], minus_one[:], ALU.pow)
+            return weight
 
         def softmax_terms(b):
             dot_exp = held.tile([P, N], F32, name=f"dot_exp{b}")
             wed_exp = held.tile([P, N], F32, name=f"wed_exp{b}")
             dot_sum_by_half = held.tile([P, HALVES], F32, name=f"dot_sum_by_half{b}")
-            dot_sum = held.tile([P, 1], F32, name=f"dot_sum{b}")
-            wed_sum = held.tile([P, 1], F32, name=f"wed_sum{b}")
+            wed_sum_by_half = held.tile([P, HALVES], F32, name=f"wed_sum_by_half{b}")
+            dot_term = held.tile([P, N], F32, name=f"dot_term{b}")
+            wed_term = held.tile([P, N], F32, name=f"wed_term{b}")
             for h in range(HALVES):
                 nc.scalar.activation(
                     dot_exp[:, half(h)], dot_ps[b][h][:], FUNC.Exp, bias=dot_shift[b][:], scale=SC,
                     accum_out=dot_sum_by_half[:, h : h + 1],
                 )
-            nc.scalar.activation(wed_exp[:], wed_score[b][:], FUNC.Exp, bias=wed_shift[b][:], accum_out=wed_sum[:])
-            nc.vector.tensor_tensor(dot_sum[:], dot_sum_by_half[:, 0:1], dot_sum_by_half[:, 1:2], ALU.add)
-            dot_term = term_of(f"dot{b}", dot_exp, dot_sum, (1.0 - MIX) * N)
-            wed_term = term_of(f"wed{b}", wed_exp, wed_sum, MIX * N)
+            for h in range(HALVES):
+                nc.scalar.activation(
+                    wed_exp[:, half(h)], wed_score[b][:, half(h)], FUNC.Exp, bias=wed_shift[b][:],
+                    accum_out=wed_sum_by_half[:, h : h + 1],
+                )
+            dot_weight = weight_of("dot", b, dot_sum_by_half, (1.0 - MIX) * N)
+            wed_weight = weight_of("wed", b, wed_sum_by_half, MIX * N)
+            if b == 0:
+                nc.vector.tensor_scalar_mul(dot_term[:], dot_exp[:], dot_weight[:])
+            else:
+                nc.scalar.activation(dot_term[:], dot_exp[:], FUNC.Copy, scale=dot_weight[:])
+            nc.vector.tensor_scalar_mul(wed_term[:], wed_exp[:], wed_weight[:])
             return dot_term, wed_term
 
         def place(b, dot_term, wed_term):

@@ -90,37 +90,19 @@ def tile_dualpathgeomattention_kernel(tc, base, q, k, offs, out):
             for h in range(HALVES):
                 nc.scalar.activation(dot_sq[b][:, half(h)], dot_ps[b][h][:], FUNC.Square)
 
-        clamped = [held.tile([P, N], F32, name=f"clamped{b}") for b in range(BLOCKS)]
-        tops = [held.tile([P, 2], F32, name=f"tops{b}") for b in range(BLOCKS)]
-        dot_shift = [held.tile([P, 1], F32, name=f"dot_shift{b}") for b in range(BLOCKS)]
-        wed_shift = [held.tile([P, 1], F32, name=f"wed_shift{b}") for b in range(BLOCKS)]
         wed_score = [held.tile([P, N], F32, name=f"wed_score{b}") for b in range(BLOCKS)]
-
-        def vector_share(b):
+        for b in range(BLOCKS):
             gram = held.tile([P, N], F32, name=f"gram{b}")
-            tops_by_half = held.tile([P, 2 * HALVES], F32, name=f"tops_by_half{b}")
+            clamped = held.tile([P, N], F32, name=f"clamped{b}")
             for h in range(HALVES):
                 nc.vector.scalar_tensor_tensor(
                     gram[:, half(h)], kn_ps[h][:], qn[:, b : b + 1], dot_sq[b][:, half(h)], ALU.mult, ALU.subtract
                 )
             for h in range(HALVES):
-                nc.vector.tensor_scalar(
-                    clamped[b][:, half(h)], gram[:, half(h)], 0.0, None, ALU.max, ALU.max,
-                    accum_out=tops_by_half[:, HALVES + h : HALVES + h + 1],
-                )
-            for h in range(HALVES):
-                nc.vector.reduce_max(tops_by_half[:, h : h + 1], dot_ps[b][h][:], axis=AXIS.X)
-            nc.vector.reduce_max(tops[b][:], tops_by_half[:].rearrange("p (t h) -> p t h", h=HALVES), axis=AXIS.X)
-            nc.vector.tensor_scalar_mul(dot_shift[b][:], tops[b][:, 0:1], -SC)
-
-        def roots(b):
-            for h in range(HALVES):
+                nc.vector.tensor_scalar_max(clamped[:, half(h)], gram[:, half(h)], 0.0)
                 nc.scalar.activation(
-                    wed_score[b][:, half(h)], clamped[b][:, half(h)], FUNC.Sqrt, bias=scaled_eps[:], scale=SC * SC
+                    wed_score[b][:, half(h)], clamped[:, half(h)], FUNC.Sqrt, bias=scaled_eps[:], scale=SC * SC
                 )
-            wed_top = held.tile([P, 1], F32, name=f"wed_top{b}")
-            nc.scalar.activation(wed_top[:], tops[b][:, 1:2], FUNC.Sqrt, bias=scaled_eps[:], scale=SC * SC)
-            nc.scalar.mul(wed_shift[b][:], wed_top[:], -1.0)
 
         def weight_of(name, b, sum_by_half, gain):
             shrunk = held.tile([P, 1], F32, name=f"{name}_shrunk{b}")
@@ -133,41 +115,41 @@ def tile_dualpathgeomattention_kernel(tc, base, q, k, offs, out):
                 nc.gpsimd.tensor_tensor(weight[:], shrunk[:], minus_one[:], ALU.pow)
             return weight
 
-        def softmax_terms(b):
+        for b in range(BLOCKS):
+            dot_top_by_half = held.tile([P, HALVES], F32, name=f"dot_top_by_half{b}")
+            dot_shift = held.tile([P, 1], F32, name=f"dot_shift{b}")
+            wed_shift = held.tile([P, 1], F32, name=f"wed_shift{b}")
+            for h in range(HALVES):
+                nc.vector.reduce_max(dot_top_by_half[:, h : h + 1], dot_ps[b][h][:], axis=AXIS.X)
+            nc.vector.tensor_scalar(
+                dot_shift[:], dot_top_by_half[:, 0:1], dot_top_by_half[:, 1:2], -SC, ALU.max, ALU.mult
+            )
+            nc.vector.reduce_max(wed_shift[:], wed_score[b][:], axis=AXIS.X, negate=True)
+
             dot_exp = held.tile([P, N], F32, name=f"dot_exp{b}")
             wed_exp = held.tile([P, N], F32, name=f"wed_exp{b}")
             dot_sum_by_half = held.tile([P, HALVES], F32, name=f"dot_sum_by_half{b}")
             wed_sum_by_half = held.tile([P, HALVES], F32, name=f"wed_sum_by_half{b}")
-            dot_term = held.tile([P, N], F32, name=f"dot_term{b}")
-            wed_term = held.tile([P, N], F32, name=f"wed_term{b}")
             for h in range(HALVES):
                 nc.scalar.activation(
-                    dot_exp[:, half(h)], dot_ps[b][h][:], FUNC.Exp, bias=dot_shift[b][:], scale=SC,
+                    dot_exp[:, half(h)], dot_ps[b][h][:], FUNC.Exp, bias=dot_shift[:], scale=SC,
                     accum_out=dot_sum_by_half[:, h : h + 1],
                 )
             for h in range(HALVES):
                 nc.scalar.activation(
-                    wed_exp[:, half(h)], wed_score[b][:, half(h)], FUNC.Exp, bias=wed_shift[b][:],
+                    wed_exp[:, half(h)], wed_score[b][:, half(h)], FUNC.Exp, bias=wed_shift[:],
                     accum_out=wed_sum_by_half[:, h : h + 1],
                 )
+
             dot_weight = weight_of("dot", b, dot_sum_by_half, (1.0 - MIX) * N)
             wed_weight = weight_of("wed", b, wed_sum_by_half, MIX * N)
+            dot_term = held.tile([P, N], F32, name=f"dot_term{b}")
+            wed_term = held.tile([P, N], F32, name=f"wed_term{b}")
+            nc.scalar.activation(dot_term[:], dot_exp[:], FUNC.Copy, scale=dot_weight[:])
             if b == 0:
-                nc.vector.tensor_scalar_mul(dot_term[:], dot_exp[:], dot_weight[:])
+                nc.vector.tensor_scalar_mul(wed_term[:], wed_exp[:], wed_weight[:])
             else:
-                nc.scalar.activation(dot_term[:], dot_exp[:], FUNC.Copy, scale=dot_weight[:])
-            nc.vector.tensor_scalar_mul(wed_term[:], wed_exp[:], wed_weight[:])
-            return dot_term, wed_term
+                nc.scalar.activation(wed_term[:], wed_exp[:], FUNC.Copy, scale=wed_weight[:])
 
-        def place(b, dot_term, wed_term):
             nc.vector.tensor_tensor(windows[b][:].indirect(offsets[:]), dot_term[:], wed_term[:], ALU.add)
             nc.sync.dma_start(out[b * P : (b + 1) * P, :], windows[b][:])
-
-        vector_share(0)
-        roots(0)
-        terms0 = softmax_terms(0)
-        vector_share(1)
-        place(0, *terms0)
-        roots(1)
-        terms1 = softmax_terms(1)
-        place(1, *terms1)

@@ -19,7 +19,6 @@ MIX = 1.0 / (1.0 + math.exp(-1.0))
 EPS = 1e-8
 
 FLOPS = 2 * C * N * E
-WARM_MATMULS = 4
 
 
 def half(h):
@@ -42,18 +41,13 @@ def tile_dualpathgeomattention_kernel(tc, base, q, k, offs, out):
         for b in range(BLOCKS):
             nc.sync.dma_start(windows[b][:], base[b * P : (b + 1) * P, :])
 
-        ones = held.tile([E, BANK], BF16, name="ones")
+        ones = held.tile([E, P], BF16, name="ones")
         scaled_eps = held.tile([P, 1], F32, name="scaled_eps")
         nc.gpsimd.memset(ones[:], 1.0)
         nc.gpsimd.memset(scaled_eps[:], SC * SC * EPS)
-        minus_one = held.tile([P, 1], F32, name="minus_one")
-        nc.gpsimd.memset(minus_one[:], -1.0)
 
         warm = held.tile([P, 1], F32, name="warm")
         nc.scalar.activation(warm[:], scaled_eps[:], FUNC.Sqrt)
-        warm_ps = psum.tile([P, BANK], F32, name="warm_ps")
-        for i in range(WARM_MATMULS):
-            nc.tensor.matmul(warm_ps[:], ones[:, 0:P], ones[:], start=True, stop=True)
 
         q_sq = held.tile([E, C], BF16, name="q_sq")
         k_sq = held.tile([E, N], BF16, name="k_sq")
@@ -79,7 +73,7 @@ def tile_dualpathgeomattention_kernel(tc, base, q, k, offs, out):
             )
         for h in range(HALVES):
             dot_product(0, h)
-            nc.tensor.matmul(kn_ps[h][:], ones[:, 0:P], k_sq[:, half(h)], start=True, stop=True)
+            nc.tensor.matmul(kn_ps[h][:], ones[:], k_sq[:, half(h)], start=True, stop=True)
         for h in range(HALVES):
             dot_product(1, h)
         qn = held.tile([P, BLOCKS], F32, name="qn")
@@ -90,66 +84,71 @@ def tile_dualpathgeomattention_kernel(tc, base, q, k, offs, out):
             for h in range(HALVES):
                 nc.scalar.activation(dot_sq[b][:, half(h)], dot_ps[b][h][:], FUNC.Square)
 
+        clamped = [held.tile([P, N], F32, name=f"clamped{b}") for b in range(BLOCKS)]
+        tops = [held.tile([P, 2], F32, name=f"tops{b}") for b in range(BLOCKS)]
+        dot_shift = [held.tile([P, 1], F32, name=f"dot_shift{b}") for b in range(BLOCKS)]
+        wed_shift = [held.tile([P, 1], F32, name=f"wed_shift{b}") for b in range(BLOCKS)]
         wed_score = [held.tile([P, N], F32, name=f"wed_score{b}") for b in range(BLOCKS)]
-        for b in range(BLOCKS):
+
+        def vector_share(b):
             gram = held.tile([P, N], F32, name=f"gram{b}")
-            clamped = held.tile([P, N], F32, name=f"clamped{b}")
+            tops_by_half = held.tile([P, 2 * HALVES], F32, name=f"tops_by_half{b}")
             for h in range(HALVES):
                 nc.vector.scalar_tensor_tensor(
                     gram[:, half(h)], kn_ps[h][:], qn[:, b : b + 1], dot_sq[b][:, half(h)], ALU.mult, ALU.subtract
                 )
             for h in range(HALVES):
-                nc.vector.tensor_scalar_max(clamped[:, half(h)], gram[:, half(h)], 0.0)
-                nc.scalar.activation(
-                    wed_score[b][:, half(h)], clamped[:, half(h)], FUNC.Sqrt, bias=scaled_eps[:], scale=SC * SC
+                nc.vector.tensor_scalar(
+                    clamped[b][:, half(h)], gram[:, half(h)], 0.0, None, ALU.max, ALU.max,
+                    accum_out=tops_by_half[:, HALVES + h : HALVES + h + 1],
                 )
-
-        def weight_of(name, b, sum_by_half, gain):
-            shrunk = held.tile([P, 1], F32, name=f"{name}_shrunk{b}")
-            weight = held.tile([P, 1], F32, name=f"{name}_weight{b}")
-            engine = nc.vector if b == 0 else nc.gpsimd
-            engine.tensor_scalar(shrunk[:], sum_by_half[:, 0:1], sum_by_half[:, 1:2], 1.0 / gain, ALU.add, ALU.mult)
-            if b == 0:
-                nc.vector.reciprocal(weight[:], shrunk[:])
-            else:
-                nc.gpsimd.tensor_tensor(weight[:], shrunk[:], minus_one[:], ALU.pow)
-            return weight
-
-        for b in range(BLOCKS):
-            dot_top_by_half = held.tile([P, HALVES], F32, name=f"dot_top_by_half{b}")
-            dot_shift = held.tile([P, 1], F32, name=f"dot_shift{b}")
-            wed_shift = held.tile([P, 1], F32, name=f"wed_shift{b}")
             for h in range(HALVES):
-                nc.vector.reduce_max(dot_top_by_half[:, h : h + 1], dot_ps[b][h][:], axis=AXIS.X)
-            nc.vector.tensor_scalar(
-                dot_shift[:], dot_top_by_half[:, 0:1], dot_top_by_half[:, 1:2], -SC, ALU.max, ALU.mult
-            )
-            nc.vector.reduce_max(wed_shift[:], wed_score[b][:], axis=AXIS.X, negate=True)
+                nc.vector.reduce_max(tops_by_half[:, h : h + 1], dot_ps[b][h][:], axis=AXIS.X)
+            nc.vector.reduce_max(tops[b][:], tops_by_half[:].rearrange("p (t h) -> p t h", h=HALVES), axis=AXIS.X)
+            nc.vector.tensor_scalar_mul(dot_shift[b][:], tops[b][:, 0:1], -SC)
 
+        def roots(b):
+            for h in range(HALVES):
+                nc.scalar.activation(
+                    wed_score[b][:, half(h)], clamped[b][:, half(h)], FUNC.Sqrt, bias=scaled_eps[:], scale=SC * SC
+                )
+            wed_top = held.tile([P, 1], F32, name=f"wed_top{b}")
+            nc.scalar.activation(wed_top[:], tops[b][:, 1:2], FUNC.Sqrt, bias=scaled_eps[:], scale=SC * SC)
+            nc.scalar.mul(wed_shift[b][:], wed_top[:], -1.0)
+
+        def term_of(name, exps, row_sum, gain):
+            inverse = held.tile([P, 1], F32, name=f"{name}_inverse")
+            term = held.tile([P, N], F32, name=f"{name}_term")
+            nc.vector.reciprocal(inverse[:], row_sum[:])
+            nc.vector.tensor_scalar(term[:], exps[:], inverse[:], gain, ALU.mult, ALU.mult)
+            return term
+
+        def softmax_terms(b):
             dot_exp = held.tile([P, N], F32, name=f"dot_exp{b}")
             wed_exp = held.tile([P, N], F32, name=f"wed_exp{b}")
             dot_sum_by_half = held.tile([P, HALVES], F32, name=f"dot_sum_by_half{b}")
-            wed_sum_by_half = held.tile([P, HALVES], F32, name=f"wed_sum_by_half{b}")
+            dot_sum = held.tile([P, 1], F32, name=f"dot_sum{b}")
+            wed_sum = held.tile([P, 1], F32, name=f"wed_sum{b}")
             for h in range(HALVES):
                 nc.scalar.activation(
-                    dot_exp[:, half(h)], dot_ps[b][h][:], FUNC.Exp, bias=dot_shift[:], scale=SC,
+                    dot_exp[:, half(h)], dot_ps[b][h][:], FUNC.Exp, bias=dot_shift[b][:], scale=SC,
                     accum_out=dot_sum_by_half[:, h : h + 1],
                 )
-            for h in range(HALVES):
-                nc.scalar.activation(
-                    wed_exp[:, half(h)], wed_score[b][:, half(h)], FUNC.Exp, bias=wed_shift[:],
-                    accum_out=wed_sum_by_half[:, h : h + 1],
-                )
+            nc.scalar.activation(wed_exp[:], wed_score[b][:], FUNC.Exp, bias=wed_shift[b][:], accum_out=wed_sum[:])
+            nc.vector.tensor_tensor(dot_sum[:], dot_sum_by_half[:, 0:1], dot_sum_by_half[:, 1:2], ALU.add)
+            dot_term = term_of(f"dot{b}", dot_exp, dot_sum, (1.0 - MIX) * N)
+            wed_term = term_of(f"wed{b}", wed_exp, wed_sum, MIX * N)
+            return dot_term, wed_term
 
-            dot_weight = weight_of("dot", b, dot_sum_by_half, (1.0 - MIX) * N)
-            wed_weight = weight_of("wed", b, wed_sum_by_half, MIX * N)
-            dot_term = held.tile([P, N], F32, name=f"dot_term{b}")
-            wed_term = held.tile([P, N], F32, name=f"wed_term{b}")
-            nc.scalar.activation(dot_term[:], dot_exp[:], FUNC.Copy, scale=dot_weight[:])
-            if b == 0:
-                nc.vector.tensor_scalar_mul(wed_term[:], wed_exp[:], wed_weight[:])
-            else:
-                nc.scalar.activation(wed_term[:], wed_exp[:], FUNC.Copy, scale=wed_weight[:])
-
+        def place(b, dot_term, wed_term):
             nc.vector.tensor_tensor(windows[b][:].indirect(offsets[:]), dot_term[:], wed_term[:], ALU.add)
             nc.sync.dma_start(out[b * P : (b + 1) * P, :], windows[b][:])
+
+        vector_share(0)
+        roots(0)
+        terms0 = softmax_terms(0)
+        vector_share(1)
+        place(0, *terms0)
+        roots(1)
+        terms1 = softmax_terms(1)
+        place(1, *terms1)

import math

import concourse.mybir as mybir

F32 = mybir.dt.float32
BF16 = mybir.dt.bfloat16
U16 = mybir.dt.uint16
ALU = mybir.AluOpType
FUNC = mybir.ActivationFunctionType
AXIS = mybir.AxisListType

P = 128
C, S, N, E = 256, 4096, 1024, 128
BLOCKS = C // P
BANK = 512
HALVES = N // BANK
SC = 1.0 / math.sqrt(E)
MIX = 1.0 / (1.0 + math.exp(-1.0))
EPS = 1e-8

FLOPS = 2 * C * N * E


def half(h):
    return slice(h * BANK, (h + 1) * BANK)


def tile_dualpathgeomattention_kernel(tc, base, q, k, offs, out):
    nc = tc.nc
    with (
        tc.tile_pool(name="held", bufs=1) as held,
        tc.psum_pool(name="psum", bufs=1) as psum,
    ):
        q_sb = held.tile([E, C], BF16, name="q_sb")
        k_sb = held.tile([E, N], BF16, name="k_sb")
        offsets = held.tile([P, N // 16], U16, name="offsets")
        nc.scalar.dma_start(k_sb[:], k)
        nc.sync.dma_start(q_sb[:], q)
        nc.sync.dma_start(offsets[:], offs)
        windows = [held.tile([P, S], F32, name=f"window{b}") for b in range(BLOCKS)]
        for b in range(BLOCKS):
            nc.sync.dma_start(windows[b][:], base[b * P : (b + 1) * P, :])

        ones = held.tile([E, P], BF16, name="ones")
        scaled_eps = held.tile([P, 1], F32, name="scaled_eps")
        nc.gpsimd.memset(ones[:], 1.0)
        nc.gpsimd.memset(scaled_eps[:], SC * SC * EPS)

        warm = held.tile([P, 1], F32, name="warm")
        nc.scalar.activation(warm[:], scaled_eps[:], FUNC.Sqrt)

        q_sq = held.tile([E, C], BF16, name="q_sq")
        k_sq = held.tile([E, N], BF16, name="k_sq")
        nc.vector.tensor_tensor(q_sq[:], q_sb[:], q_sb[:], ALU.mult)
        for h in range(HALVES):
            nc.vector.tensor_tensor(k_sq[:, half(h)], k_sb[:, half(h)], k_sb[:, half(h)], ALU.mult)

        qn_ps = psum.tile([P, BLOCKS], F32, name="qn_ps")
        kn_ps = [psum.tile([P, BANK], F32, name=f"kn_ps{h}") for h in range(HALVES)]
        dot_ps = [
            [psum.tile([P, BANK], F32, name=f"dot_ps{b}{h}") for h in range(HALVES)]
            for b in range(BLOCKS)
        ]

        def dot_product(b, h):
            nc.tensor.matmul(
                dot_ps[b][h][:], q_sb[:, b * P : (b + 1) * P], k_sb[:, half(h)], start=True, stop=True
            )

        for b in range(BLOCKS):
            nc.tensor.matmul(
                qn_ps[:, b : b + 1], q_sq[:, b * P : (b + 1) * P], ones[:, 0:1], start=True, stop=True
            )
        for h in range(HALVES):
            dot_product(0, h)
            nc.tensor.matmul(kn_ps[h][:], ones[:], k_sq[:, half(h)], start=True, stop=True)
        for h in range(HALVES):
            dot_product(1, h)
        qn = held.tile([P, BLOCKS], F32, name="qn")
        nc.vector.tensor_copy(qn[:], qn_ps[:])

        dot_sq = [held.tile([P, N], F32, name=f"dot_sq{b}") for b in range(BLOCKS)]
        for b in range(BLOCKS):
            for h in range(HALVES):
                nc.scalar.activation(dot_sq[b][:, half(h)], dot_ps[b][h][:], FUNC.Square)

        clamped = [held.tile([P, N], F32, name=f"clamped{b}") for b in range(BLOCKS)]
        tops = [held.tile([P, 2], F32, name=f"tops{b}") for b in range(BLOCKS)]
        dot_shift = [held.tile([P, 1], F32, name=f"dot_shift{b}") for b in range(BLOCKS)]
        wed_shift = [held.tile([P, 1], F32, name=f"wed_shift{b}") for b in range(BLOCKS)]
        wed_score = [held.tile([P, N], F32, name=f"wed_score{b}") for b in range(BLOCKS)]

        def vector_share(b):
            gram = held.tile([P, N], F32, name=f"gram{b}")
            tops_by_half = held.tile([P, 2 * HALVES], F32, name=f"tops_by_half{b}")
            for h in range(HALVES):
                nc.vector.scalar_tensor_tensor(
                    gram[:, half(h)], kn_ps[h][:], qn[:, b : b + 1], dot_sq[b][:, half(h)], ALU.mult, ALU.subtract
                )
            for h in range(HALVES):
                nc.vector.tensor_scalar(
                    clamped[b][:, half(h)], gram[:, half(h)], 0.0, None, ALU.max, ALU.max,
                    accum_out=tops_by_half[:, HALVES + h : HALVES + h + 1],
                )
            for h in range(HALVES):
                nc.vector.reduce_max(tops_by_half[:, h : h + 1], dot_ps[b][h][:], axis=AXIS.X)
            nc.vector.reduce_max(tops[b][:], tops_by_half[:].rearrange("p (t h) -> p t h", h=HALVES), axis=AXIS.X)
            nc.vector.tensor_scalar_mul(dot_shift[b][:], tops[b][:, 0:1], -SC)

        def roots(b):
            for h in range(HALVES):
                nc.scalar.activation(
                    wed_score[b][:, half(h)], clamped[b][:, half(h)], FUNC.Sqrt, bias=scaled_eps[:], scale=SC * SC
                )
            wed_top = held.tile([P, 1], F32, name=f"wed_top{b}")
            nc.scalar.activation(wed_top[:], tops[b][:, 1:2], FUNC.Sqrt, bias=scaled_eps[:], scale=SC * SC)
            nc.scalar.mul(wed_shift[b][:], wed_top[:], -1.0)

        def term_of(name, exps, row_sum, gain):
            inverse = held.tile([P, 1], F32, name=f"{name}_inverse")
            term = held.tile([P, N], F32, name=f"{name}_term")
            nc.vector.reciprocal(inverse[:], row_sum[:])
            nc.vector.tensor_scalar(term[:], exps[:], inverse[:], gain, ALU.mult, ALU.mult)
            return term

        def softmax_terms(b):
            dot_exp = held.tile([P, N], F32, name=f"dot_exp{b}")
            wed_exp = held.tile([P, N], F32, name=f"wed_exp{b}")
            dot_sum_by_half = held.tile([P, HALVES], F32, name=f"dot_sum_by_half{b}")
            dot_sum = held.tile([P, 1], F32, name=f"dot_sum{b}")
            wed_sum = held.tile([P, 1], F32, name=f"wed_sum{b}")
            for h in range(HALVES):
                nc.scalar.activation(
                    dot_exp[:, half(h)], dot_ps[b][h][:], FUNC.Exp, bias=dot_shift[b][:], scale=SC,
                    accum_out=dot_sum_by_half[:, h : h + 1],
                )
            nc.scalar.activation(wed_exp[:], wed_score[b][:], FUNC.Exp, bias=wed_shift[b][:], accum_out=wed_sum[:])
            nc.vector.tensor_tensor(dot_sum[:], dot_sum_by_half[:, 0:1], dot_sum_by_half[:, 1:2], ALU.add)
            dot_term = term_of(f"dot{b}", dot_exp, dot_sum, (1.0 - MIX) * N)
            wed_term = term_of(f"wed{b}", wed_exp, wed_sum, MIX * N)
            return dot_term, wed_term

        def place(b, dot_term, wed_term):
            nc.vector.tensor_tensor(windows[b][:].indirect(offsets[:]), dot_term[:], wed_term[:], ALU.add)
            nc.sync.dma_start(out[b * P : (b + 1) * P, :], windows[b][:])

        vector_share(0)
        roots(0)
        terms0 = softmax_terms(0)
        vector_share(1)
        place(0, *terms0)
        roots(1)
        terms1 = softmax_terms(1)
        place(1, *terms1)
